import numpy as np
import ml_dtypes


def mxq(x, axis, fmt="e4m3"):
    dtype, down = {"e4m3": (ml_dtypes.float8_e4m3fn, 7), "e5m2": (ml_dtypes.float8_e5m2, 14)}[fmt]
    v = np.moveaxis(np.asarray(x, np.float32).astype(ml_dtypes.bfloat16).astype(np.float64), axis, -1)
    blocks = v.reshape(v.shape[:-1] + (-1, 32))
    amax = np.abs(blocks).max(-1, keepdims=True)
    byte = np.maximum(np.where(amax > 0, np.frexp(amax)[1] - 1 + 127, 0) - down, 1)
    scale = np.exp2(byte - 127.0)
    codes = (blocks / scale).astype(np.float32).astype(dtype).astype(np.float64)
    return np.moveaxis((codes * scale).reshape(v.shape), -1, axis)


WIDE = False


def mx_kscale(k):
    if not WIDE:
        return np.ones(k)
    levels = np.array([10, -10, 5, -5, 0])
    if k % 512:
        return np.exp2(np.random.permutation(np.resize(levels, k // 32))).repeat(32)
    a = np.empty((k // 512, 16))
    for p in range(k // 512):
        a[p, :8] = np.random.permutation(np.resize(levels, 8))
        for g in range(8):
            far = levels[np.abs(levels - a[p, g]) >= 10]
            a[p, g + 8] = far[np.random.randint(len(far))]
    return np.exp2(a.ravel()).repeat(32)


BF16 = ml_dtypes.bfloat16


def bf(x):
    return np.asarray(x, np.float32).astype(BF16)


def f64(x):
    return np.asarray(x).astype(np.float64)


B, S, D, F, P, NQ = 2, 128, 1024, 1024, 1024, 3
LN_EPS = 1e-5


def layernorm(v, g, b):
    m = v.mean(-1, keepdims=True)
    var = v.var(-1, keepdims=True)
    return (v - m) / np.sqrt(var + LN_EPS) * g + b


def setup_inputs():
    s = mx_kscale(P)
    return {"in_proto": bf(np.random.standard_normal((NQ, F, P)) * s),
            "pt_w": bf(np.random.standard_normal((NQ, D, P)) / np.sqrt(P) / s),
            "pln_g": bf(1.0 + 0.1 * np.random.standard_normal((NQ, D))),
            "pln_b": bf(0.1 * np.random.standard_normal((NQ, D))),
            "proto_w": bf(np.random.standard_normal((NQ, F, D)) * 0.5)}


def reference(in_proto, pt_w, pln_g, pln_b, proto_w):
    prc = mxq(f64(in_proto), 2, "e4m3") @ mxq(f64(pt_w), 2, "e4m3").transpose(0, 2, 1)
    return f64(proto_w) + layernorm(prc, f64(pln_g)[:, None, :], f64(pln_b)[:, None, :])

@@ -1,0 +1,291 @@
+from contextlib import ExitStack
+
+import concourse.mybir as mybir
+from concourse.masks import make_identity
+
+F32 = mybir.dt.float32
+BF16 = mybir.dt.bfloat16
+U32 = mybir.dt.uint32
+U8 = mybir.dt.uint8
+I32 = mybir.dt.int32
+FP8X4 = mybir.dt.float8_e4m3fn_x4
+ACT = mybir.ActivationFunctionType
+ALU = mybir.AluOpType
+
+NB = 3
+D = 1024
+P = 128
+H = 512
+LN_EPS = 1e-5
+FLOPS = 2 * NB * D * D * D
+
+N_SLOTS = 8 * NB
+N_UNITS = 8 * NB
+HEAD_UNITS = 6
+PE_C_SLOTS = tuple(range(4, 17))
+EARLY_C_SLOTS = (0, 1, 2, 3)
+B_SLOTS = {2: (1, 1), 3: (1, 0), 10: (2, 1), 11: (2, 0)}
+
+
+def units_of_slot(s):
+    if s == 0:
+        return [6, 7]
+    return [s + 7] if s + 7 < N_UNITS else []
+
+
+def tile_moietransformerblock_pb_kernel(tc, in_proto, pt_w, pln_g, pln_b, proto_w, out):
+    nc = tc.nc
+    a_view = in_proto.rearrange("n (p t) k -> n p t k", t=8)
+    w_view = pt_w.rearrange("n (t p) k -> n p t k", p=P)
+    pw_view = proto_w.rearrange("n (p t) d -> n p t d", t=8)
+    out_view = out.rearrange("n (p t) d -> n p t d", t=8)
+
+    with ExitStack() as ctx:
+        ctx.enter_context(tc.manual_schedule())
+        const = ctx.enter_context(tc.tile_pool(name="const", bufs=1))
+        rawp = ctx.enter_context(tc.tile_pool(name="rawp", bufs=4))
+        pwp = ctx.enter_context(tc.tile_pool(name="pwp", bufs=3))
+        grpp = ctx.enter_context(tc.tile_pool(name="grpp", bufs=4))
+        codep = ctx.enter_context(tc.tile_pool(name="codep", bufs=2))
+        xsp = ctx.enter_context(tc.tile_pool(name="xsp", bufs=3))
+        tpool = ctx.enter_context(tc.tile_pool(name="tpool", bufs=5))
+        capool = ctx.enter_context(tc.tile_pool(name="capool", bufs=5))
+        cbpool = ctx.enter_context(tc.tile_pool(name="cbpool", bufs=2))
+        smallp = ctx.enter_context(tc.tile_pool(name="smallp", bufs=4))
+        psum_t = ctx.enter_context(tc.psum_pool(name="psum_t", bufs=2))
+        psum_c = ctx.enter_context(tc.psum_pool(name="psum_c", bufs=2))
+        psum_x = ctx.enter_context(tc.psum_pool(name="psum_x", bufs=2))
+        psum_g = ctx.enter_context(tc.psum_pool(name="psum_g", bufs=2))
+        tr_homes = ((psum_t, "tr"), (psum_x, "x"), (psum_c, "cps"))
+
+        gpad = const.tile([P, NB * D], BF16, name="gpad")
+        bpad = const.tile([P, NB * D], BF16, name="bpad")
+        nc.vector.memset(gpad[:].bitcast(I32), 0)
+        nc.scalar.dma_start(out=gpad[0:1, :], in_=pln_g.rearrange("(o n) d -> o (n d)", o=1))
+        nc.vector.memset(bpad[:].bitcast(I32), 0)
+        nc.scalar.dma_start(out=bpad[0:1, :], in_=pln_b.rearrange("(o n) d -> o (n d)", o=1))
+        ident = const.tile([P, P], F32, name="ident")
+        make_identity(nc, ident[:])
+        identb = const.tile([P, P], BF16, name="identb")
+        make_identity(nc, identb[:])
+        eps = const.tile([P, 1], F32, name="eps")
+        nc.vector.memset(eps[:], LN_EPS)
+        warm = const.tile([P, 1], F32, name="warm")
+        nc.scalar.activation(out=warm[:], in_=eps[:], func=ACT.Abs_reciprocal_sqrt, bias=eps[:], scale=1.0)
+        ones = const.tile([P, P], BF16, name="ones")
+        nc.vector.memset(ones[:], 1.0)
+        b_all = const.tile([P, NB * D], BF16, name="b_all")
+        junk = const.tile([P, D], BF16, name="junk")
+        junk2 = const.tile([P, 2], F32, name="junk2")
+
+        raw = {}
+        pw_raw = {}
+        codes = {}
+        ca_tiles = {}
+        cb_tiles = {}
+        cps_tiles = {}
+        state = {}
+        unit = {}
+
+        def load_chunk(c):
+            n, r = divmod(c, 4)
+            view = w_view if r < 2 else a_view
+            j = r % 2
+            t_raw = rawp.tile([P, 4 * D], BF16, name="raw%d" % c, tag="raw")
+            nc.sync.dma_start(
+                out=t_raw[:].rearrange("p (t k) -> p t k", t=4),
+                in_=view[n][:, 4 * j : 4 * j + 4, :],
+            )
+            raw[c] = t_raw
+
+        def load_pw(k):
+            n, j = divmod(k, 2)
+            t_pw = pwp.tile([P, 4 * D], BF16, name="pw%d" % k, tag="pw")
+            nc.sync.dma_start(
+                out=t_pw[:].rearrange("p (t k) -> p t k", t=4),
+                in_=pw_view[n][:, 4 * j : 4 * j + 4, :],
+            )
+            pw_raw[k] = t_pw
+
+        def broadcast_b(n, h):
+            cols = slice(n * D + H * h, n * D + H * h + H)
+            ps = psum_t.tile([P, H], F32, name="bc", tag="tr")
+            nc.tensor.matmul(ps[:], lhsT=ones[:], rhs=bpad[:, cols], start=True, stop=True)
+            nc.scalar.copy(out=b_all[:, cols], in_=ps[:])
+
+        def broadcast_g(n):
+            tiles = []
+            for h in range(2):
+                cols = slice(n * D + H * h, n * D + H * h + H)
+                g_h = psum_g.tile([P, H], F32, name="gps", tag="gps")
+                nc.tensor.matmul(g_h[:], lhsT=ones[:], rhs=gpad[:, cols], start=True, stop=True)
+                tiles.append(g_h)
+            return tiles
+
+        def unit_front(u, home):
+            c, g = divmod(u, 2)
+            n, r = divmod(c, 4)
+            op = 0 if r < 2 else 1
+            j = r % 2
+            if (n, op) not in codes:
+                cd = codep.tile([P, 2, D], U32, name="cd%d_%d" % (n, op), tag="cd%d" % op, align_bytes=64)
+                sc = codep.tile([P, 2, D], U8, name="sc%d_%d" % (n, op), tag="sc%d" % op, align_bytes=64)
+                codes[(n, op)] = (cd, sc)
+            pool, tag = tr_homes[home]
+            words = raw[c][:].bitcast(F32)
+            grp = grpp.tile([P, 2048], BF16, name="grp%d" % u, tag="grp", align_bytes=64)
+            grp_w = grp[:].bitcast(F32).rearrange("p (a r w) -> p a r w", a=4, w=2)
+            for h in range(2):
+                ps = pool.tile([P, 2, 2, P], F32, name="tr", tag=tag)
+                for tl in range(2):
+                    for w in range(2):
+                        col = H * (2 * h + tl) + 256 * g
+                        nc.tensor.transpose(ps[:, tl, w, :], words[:, col + w : col + 256 : 2], ident[:])
+                src = ps[:].rearrange("p a w r -> p a r w")
+                dst = grp_w[:, 2 * h : 2 * h + 2]
+                if h == 1:
+                    nc.vector.tensor_copy(out=dst, in_=src)
+                else:
+                    nc.scalar.copy(out=dst, in_=src)
+            if g == 1 and c + 4 < 4 * NB:
+                load_chunk(c + 4)
+            unit[u] = (n, op, g, j, grp)
+
+        def unit_back(u):
+            n, op, g, j, grp = unit[u]
+            cd, sc = codes[(n, op)]
+            cols = slice(H * j, H * j + H)
+            nc.vector.quantize_mx(out=cd[:, g, cols].bitcast(FP8X4), scales=sc[:, g, cols], in_=grp[:])
+
+        def make_ca(s):
+            n = s // 8
+            k, tl = divmod(s, 4)
+            c_t = capool.tile([P, H], F32, name="ca%d" % s, tag="ca")
+            nc.vector.tensor_tensor(
+                out=c_t[:], in0=pw_raw[k][:, tl * D : tl * D + H], in1=b_all[:, n * D : n * D + H], op=ALU.add
+            )
+            ca_tiles[s] = c_t
+
+        def make_cb(s):
+            n = s // 8
+            k, tl = divmod(s, 4)
+            c_t = cbpool.tile([P, H], F32, name="cb%d" % s, tag="cb")
+            nc.gpsimd.tensor_tensor(
+                out=c_t[:], in0=pw_raw[k][:, tl * D + H : (tl + 1) * D], in1=b_all[:, n * D + H : (n + 1) * D], op=ALU.add
+            )
+            cb_tiles[s] = c_t
+
+        def make_c_pe(s):
+            n = s // 8
+            k, tl = divmod(s, 4)
+            c_ps = psum_c.tile([P, H], F32, name="cps", tag="cps")
+            nc.tensor.matmul(c_ps[:], lhsT=identb[:], rhs=pw_raw[k][:, tl * D : tl * D + H], start=True, stop=False)
+            nc.tensor.matmul(c_ps[:], lhsT=ones[:], rhs=bpad[:, n * D : n * D + H], start=False, stop=True)
+            cps_tiles[s] = c_ps
+
+        def finish_b(s):
+            t_t, rstd = state[s]
+            nc.vector.scalar_tensor_tensor(
+                out=t_t[:, H:D], in0=t_t[:, H:D], scalar=rstd[:], in1=cb_tiles[s][:], op0=ALU.mult, op1=ALU.add
+            )
+
+        def finish_a(s):
+            n, i = divmod(s, 8)
+            t_t, rstd = state[s]
+            c_a = cps_tiles[s] if s in PE_C_SLOTS else ca_tiles[s]
+            nc.vector.scalar_tensor_tensor(
+                out=t_t[:, 0:H], in0=t_t[:, 0:H], scalar=rstd[:], in1=c_a[:], op0=ALU.mult, op1=ALU.add
+            )
+            nc.sync.dma_start(out=out_view[n][:, i, :], in_=t_t[:])
+
+        def make_rstd(s):
+            t_t, ssq = state[s]
+            rstd = smallp.tile([P, 1], F32, name="rstd%d" % s, tag="rstd")
+            nc.scalar.activation(out=rstd[:], in_=ssq[:], func=ACT.Abs_reciprocal_sqrt, bias=eps[:], scale=1.0 / D)
+            state[s] = (t_t, rstd)
+
+        load_chunk(0)
+        load_chunk(1)
+        load_chunk(2)
+        load_pw(0)
+        load_chunk(3)
+        for u in range(HEAD_UNITS):
+            unit_front(u, u % 3)
+            if 0 < u < HEAD_UNITS - 1:
+                unit_back(u - 1)
+            if u >= HEAD_UNITS - 2:
+                unit_back(u)
+            if u == 3:
+                load_pw(1)
+        g_ps = broadcast_g(0)
+        broadcast_b(0, 1)
+        broadcast_b(0, 0)
+        make_cb(0)
+        waiting = []
+
+        for s in range(N_SLOTS):
+            n, i = divmod(s, 8)
+            cd_w, sc_w = codes[(n, 0)]
+            cd_a, sc_a = codes[(n, 1)]
+            rows = slice(P * i, P * i + P)
+            xs = xsp.tile([P, D], F32, name="xs%d" % s, tag="xs")
+            sums = smallp.tile([P, 2], F32, name="sums%d" % s, tag="sums")
+            x_ps = []
+            for h in range(2):
+                cols = slice(H * h, H * h + H)
+                x_h = psum_x.tile([P, H], F32, name="x", tag="x")
+                for g in range(2):
+                    nc.tensor.matmul_mx(
+                        out=x_h[:],
+                        lhsT=cd_a[:, g, rows].bitcast(FP8X4),
+                        lhsT_scale=sc_a[:, g, rows],
+                        rhs=cd_w[:, g, cols].bitcast(FP8X4),
+                        rhs_scale=sc_w[:, g, cols],
+                        start=(g == 0),
+                        stop=(g == 1),
+                    )
+                x_ps.append(x_h)
+            if s == 0:
+                for e in EARLY_C_SLOTS:
+                    make_ca(e)
+            nc.scalar.activation(out=xs[:, 0:H], in_=x_ps[0][:], func=ACT.Copy, accum_out=sums[:, 0:1])
+            if s > 0:
+                make_rstd(s - 1)
+            nc.scalar.activation(out=xs[:, H:D], in_=x_ps[1][:], func=ACT.Copy, accum_out=sums[:, 1:2])
+            if s > 0:
+                finish_b(s - 1)
+            for u in waiting:
+                unit_back(u)
+            if s + 1 < N_SLOTS:
+                make_cb(s + 1)
+                if s + 1 not in PE_C_SLOTS and s + 1 not in EARLY_C_SLOTS:
+                    make_ca(s + 1)
+            if s > 0:
+                if s - 1 in PE_C_SLOTS:
+                    make_c_pe(s - 1)
+                finish_a(s - 1)
+            waiting = units_of_slot(s)
+            for k, u in enumerate(waiting):
+                unit_front(u, 2 * k)
+            if s > 0 and i == 0:
+                g_ps = broadcast_g(n)
+            negmean = smallp.tile([P, 1], F32, name="nm%d" % s, tag="nm")
+            nc.scalar.activation(out=junk2[:], in_=sums[:], func=ACT.Copy, scale=-1.0 / D, accum_out=negmean[:])
+            t_t = tpool.tile([P, D], F32, name="t%d" % s, tag="t")
+            for h in (1, 0):
+                cols = slice(H * h, H * h + H)
+                nc.vector.scalar_tensor_tensor(
+                    out=t_t[:, cols], in0=xs[:, cols], scalar=negmean[:], in1=g_ps[h][:], op0=ALU.add, op1=ALU.mult
+                )
+            ssq = smallp.tile([P, 1], F32, name="ssq%d" % s, tag="ssq")
+            nc.scalar.activation(out=junk[:], in_=xs[:], func=ACT.Square, bias=negmean[:], scale=1.0, accum_out=ssq[:])
+            state[s] = (t_t, ssq)
+            if s in B_SLOTS:
+                broadcast_b(B_SLOTS[s][0], B_SLOTS[s][1])
+            if s == 1:
+                load_pw(2)
+            if s >= 4 and s % 4 == 0 and s // 4 + 2 < 2 * NB:
+                load_pw(s // 4 + 2)
+        make_rstd(N_SLOTS - 1)
+        finish_b(N_SLOTS - 1)
+        finish_a(N_SLOTS - 1)

@@ -20,17 +20,19 @@ LN_EPS = 1e-5
 FLOPS = 2 * NB * D * D * D
 
 N_SLOTS = 8 * NB
-N_UNITS = 8 * NB
-HEAD_UNITS = 6
-PE_C_SLOTS = tuple(range(4, 17))
-EARLY_C_SLOTS = (0, 1, 2, 3)
-B_SLOTS = {2: (1, 1), 3: (1, 0), 10: (2, 1), 11: (2, 0)}
+CUT = 336
 
 
-def units_of_slot(s):
-    if s == 0:
-        return [6, 7]
-    return [s + 7] if s + 7 < N_UNITS else []
+def prep_units():
+    units = []
+    for n in range(NB):
+        a = [("a", n, q) for q in (1, 2, 3)]
+        if n + 1 < NB:
+            w = [("w", n + 1, j, g) for j in range(2) for g in range(2)]
+            units += [a[0], a[1], w[0], w[1], a[2], w[2], w[3], ("a", n + 1, 0)]
+        else:
+            units += a
+    return units
 
 
 def tile_moietransformerblock_pb_kernel(tc, in_proto, pt_w, pln_g, pln_b, proto_w, out):
@@ -43,13 +45,13 @@ def tile_moietransformerblock_pb_kernel(tc, in_proto, pt_w, pln_g, pln_b, proto_
     with ExitStack() as ctx:
         ctx.enter_context(tc.manual_schedule())
         const = ctx.enter_context(tc.tile_pool(name="const", bufs=1))
-        rawp = ctx.enter_context(tc.tile_pool(name="rawp", bufs=4))
+        headp = ctx.enter_context(tc.tile_pool(name="headp", bufs=8))
+        rawp = ctx.enter_context(tc.tile_pool(name="rawp", bufs=5))
         pwp = ctx.enter_context(tc.tile_pool(name="pwp", bufs=3))
         grpp = ctx.enter_context(tc.tile_pool(name="grpp", bufs=4))
         codep = ctx.enter_context(tc.tile_pool(name="codep", bufs=2))
         xsp = ctx.enter_context(tc.tile_pool(name="xsp", bufs=3))
-        tpool = ctx.enter_context(tc.tile_pool(name="tpool", bufs=5))
-        capool = ctx.enter_context(tc.tile_pool(name="capool", bufs=5))
+        tpool = ctx.enter_context(tc.tile_pool(name="tpool", bufs=8))
         cbpool = ctx.enter_context(tc.tile_pool(name="cbpool", bufs=2))
         smallp = ctx.enter_context(tc.tile_pool(name="smallp", bufs=4))
         psum_t = ctx.enter_context(tc.psum_pool(name="psum_t", bufs=2))
@@ -58,45 +60,25 @@ def tile_moietransformerblock_pb_kernel(tc, in_proto, pt_w, pln_g, pln_b, proto_
         psum_g = ctx.enter_context(tc.psum_pool(name="psum_g", bufs=2))
         tr_homes = ((psum_t, "tr"), (psum_x, "x"), (psum_c, "cps"))
 
-        gpad = const.tile([P, NB * D], BF16, name="gpad")
-        bpad = const.tile([P, NB * D], BF16, name="bpad")
-        nc.vector.memset(gpad[:].bitcast(I32), 0)
-        nc.scalar.dma_start(out=gpad[0:1, :], in_=pln_g.rearrange("(o n) d -> o (n d)", o=1))
-        nc.vector.memset(bpad[:].bitcast(I32), 0)
-        nc.scalar.dma_start(out=bpad[0:1, :], in_=pln_b.rearrange("(o n) d -> o (n d)", o=1))
-        ident = const.tile([P, P], F32, name="ident")
-        make_identity(nc, ident[:])
-        identb = const.tile([P, P], BF16, name="identb")
-        make_identity(nc, identb[:])
-        eps = const.tile([P, 1], F32, name="eps")
-        nc.vector.memset(eps[:], LN_EPS)
-        warm = const.tile([P, 1], F32, name="warm")
-        nc.scalar.activation(out=warm[:], in_=eps[:], func=ACT.Abs_reciprocal_sqrt, bias=eps[:], scale=1.0)
-        ones = const.tile([P, P], BF16, name="ones")
-        nc.vector.memset(ones[:], 1.0)
-        b_all = const.tile([P, NB * D], BF16, name="b_all")
-        junk = const.tile([P, D], BF16, name="junk")
-        junk2 = const.tile([P, 2], F32, name="junk2")
-
         raw = {}
         pw_raw = {}
         codes = {}
-        ca_tiles = {}
         cb_tiles = {}
         cps_tiles = {}
         state = {}
         unit = {}
 
-        def load_chunk(c):
-            n, r = divmod(c, 4)
-            view = w_view if r < 2 else a_view
-            j = r % 2
-            t_raw = rawp.tile([P, 4 * D], BF16, name="raw%d" % c, tag="raw")
-            nc.sync.dma_start(
-                out=t_raw[:].rearrange("p (t k) -> p t k", t=4),
-                in_=view[n][:, 4 * j : 4 * j + 4, :],
-            )
-            raw[c] = t_raw
+        def load_pair(op, q):
+            view = w_view if op == 0 else a_view
+            t_raw = headp.tile([P, 2 * D], BF16, name="h%d_%d" % (op, q), tag="h")
+            nc.sync.dma_start(out=t_raw[:].rearrange("p (t k) -> p t k", t=2), in_=view[0][:, 2 * q : 2 * q + 2, :])
+            raw[("h", op, q)] = t_raw
+
+        def load_chunk(op, n, j):
+            view = w_view if op == 0 else a_view
+            t_raw = rawp.tile([P, 4 * D], BF16, name="raw%d_%d_%d" % (op, n, j), tag="raw")
+            nc.sync.dma_start(out=t_raw[:].rearrange("p (t k) -> p t k", t=4), in_=view[n][:, 4 * j : 4 * j + 4, :])
+            raw[(op, n, j)] = t_raw
 
         def load_pw(k):
             n, j = divmod(k, 2)
@@ -107,96 +89,135 @@ def tile_moietransformerblock_pb_kernel(tc, in_proto, pt_w, pln_g, pln_b, proto_
             )
             pw_raw[k] = t_pw
 
-        def broadcast_b(n, h):
-            cols = slice(n * D + H * h, n * D + H * h + H)
-            ps = psum_t.tile([P, H], F32, name="bc", tag="tr")
-            nc.tensor.matmul(ps[:], lhsT=ones[:], rhs=bpad[:, cols], start=True, stop=True)
-            nc.scalar.copy(out=b_all[:, cols], in_=ps[:])
+        load_pair(0, 0)
+        load_pair(0, 1)
+        gb = const.tile([P, D], BF16, name="gb")
+        nc.vector.memset(gb[:].bitcast(I32), 0)
+        nc.sync.dma_start(out=gb[0:NB, :], in_=pln_g)
+        nc.sync.dma_start(out=gb[NB : 2 * NB, :], in_=pln_b)
+        load_pair(0, 2)
+        load_pair(0, 3)
+        load_pair(1, 0)
+        load_pair(1, 1)
+        b_all = const.tile([P, NB, D - CUT], BF16, name="b_all")
+        load_pair(1, 2)
+        nc.sync.dma_start(out=b_all[:, 0, :], in_=pln_b[0, CUT:D].partition_broadcast(P))
+        load_pw(0)
+        load_chunk(0, 1, 0)
+        load_pair(1, 3)
+        load_chunk(0, 1, 1)
+        load_pw(1)
+        for n in range(1, NB):
+            nc.sync.dma_start(out=b_all[:, n, :], in_=pln_b[n, CUT:D].partition_broadcast(P))
+        load_chunk(1, 1, 0)
+        load_chunk(1, 1, 1)
+        load_pw(2)
+        load_chunk(0, 2, 0)
+        ident = const.tile([P, P], F32, name="ident")
+        make_identity(nc, ident[:])
+        identb = const.tile([P, P], BF16, name="identb")
+        make_identity(nc, identb[:])
+        eps = const.tile([P, 1], F32, name="eps")
+        nc.vector.memset(eps[:], LN_EPS)
+        warm = const.tile([P, 1], F32, name="warm")
+        nc.scalar.activation(out=warm[:], in_=eps[:], func=ACT.Abs_reciprocal_sqrt, bias=eps[:], scale=1.0)
+        sel = const.tile([P, 2 * NB, P], BF16, name="sel")
+        for r in range(2 * NB):
+            nc.vector.tensor_copy(out=sel[:, r, :], in_=identb[:, r : r + 1].to_broadcast([P, P]))
+        junk = const.tile([P, D], BF16, name="junk")
+        junk2 = const.tile([P, 2], F32, name="junk2")
 
         def broadcast_g(n):
             tiles = []
             for h in range(2):
-                cols = slice(n * D + H * h, n * D + H * h + H)
                 g_h = psum_g.tile([P, H], F32, name="gps", tag="gps")
-                nc.tensor.matmul(g_h[:], lhsT=ones[:], rhs=gpad[:, cols], start=True, stop=True)
+                nc.tensor.matmul(g_h[:], lhsT=sel[:, n, :], rhs=gb[:, H * h : H * h + H], start=True, stop=True)
                 tiles.append(g_h)
             return tiles
 
-        def unit_front(u, home):
-            c, g = divmod(u, 2)
-            n, r = divmod(c, 4)
-            op = 0 if r < 2 else 1
-            j = r % 2
-            if (n, op) not in codes:
-                cd = codep.tile([P, 2, D], U32, name="cd%d_%d" % (n, op), tag="cd%d" % op, align_bytes=64)
-                sc = codep.tile([P, 2, D], U8, name="sc%d_%d" % (n, op), tag="sc%d" % op, align_bytes=64)
-                codes[(n, op)] = (cd, sc)
+        def code_tiles(op, n):
+            if (op, n) not in codes:
+                cd = codep.tile([P, 2 * D], U32, name="cd%d_%d" % (op, n), tag="cd%d" % op, align_bytes=64)
+                sc = codep.tile([P, 2 * D], U8, name="sc%d_%d" % (op, n), tag="sc%d" % op, align_bytes=64)
+                codes[(op, n)] = (cd, sc)
+            return codes[(op, n)]
+
+        def unit_front(u, home, v_copies):
             pool, tag = tr_homes[home]
-            words = raw[c][:].bitcast(F32)
-            grp = grpp.tile([P, 2048], BF16, name="grp%d" % u, tag="grp", align_bytes=64)
+            if u[0] == "w":
+                words = raw[(0, u[1], u[2])][:].bitcast(F32)
+                starts = [[H * (2 * h + tl) + 256 * u[3] for tl in range(2)] for h in range(2)]
+            elif u[0] == "a" and u[1] > 0:
+                words = raw[(1, u[1], u[2] // 2)][:].bitcast(F32)
+                starts = [[H * (2 * (u[2] % 2) + tl) + 256 * h for tl in range(2)] for h in range(2)]
+            else:
+                words = raw[("h", 0 if u[0] == "w0" else 1, u[2])][:].bitcast(F32)
+                starts = [[H * tl + 256 * h for tl in range(2)] for h in range(2)]
+            grp = grpp.tile([P, 2048], BF16, name="grp", tag="grp", align_bytes=64)
             grp_w = grp[:].bitcast(F32).rearrange("p (a r w) -> p a r w", a=4, w=2)
             for h in range(2):
                 ps = pool.tile([P, 2, 2, P], F32, name="tr", tag=tag)
                 for tl in range(2):
                     for w in range(2):
-                        col = H * (2 * h + tl) + 256 * g
+                        col = starts[h][tl]
                         nc.tensor.transpose(ps[:, tl, w, :], words[:, col + w : col + 256 : 2], ident[:])
                 src = ps[:].rearrange("p a w r -> p a r w")
                 dst = grp_w[:, 2 * h : 2 * h + 2]
-                if h == 1:
+                if h in v_copies:
                     nc.vector.tensor_copy(out=dst, in_=src)
                 else:
                     nc.scalar.copy(out=dst, in_=src)
-            if g == 1 and c + 4 < 4 * NB:
-                load_chunk(c + 4)
-            unit[u] = (n, op, g, j, grp)
+            unit[u] = grp
+
+        def quantize(op, n, cols, in_):
+            cd, sc = code_tiles(op, n)
+            nc.vector.quantize_mx(out=cd[:, cols].bitcast(FP8X4), scales=sc[:, cols], in_=in_)
 
         def unit_back(u):
-            n, op, g, j, grp = unit[u]
-            cd, sc = codes[(n, op)]
-            cols = slice(H * j, H * j + H)
-            nc.vector.quantize_mx(out=cd[:, g, cols].bitcast(FP8X4), scales=sc[:, g, cols], in_=grp[:])
-
-        def make_ca(s):
-            n = s // 8
-            k, tl = divmod(s, 4)
-            c_t = capool.tile([P, H], F32, name="ca%d" % s, tag="ca")
-            nc.vector.tensor_tensor(
-                out=c_t[:], in0=pw_raw[k][:, tl * D : tl * D + H], in1=b_all[:, n * D : n * D + H], op=ALU.add
-            )
-            ca_tiles[s] = c_t
+            grp = unit[u]
+            if u[0] == "w":
+                lo = D * u[3] + H * u[2]
+                quantize(0, u[1], slice(lo, lo + H), grp[:])
+            elif u[0] == "a":
+                quantize(1, u[1], slice(H * u[2], H * u[2] + H), grp[:])
+            else:
+                for g in range(2):
+                    lo = D * g + 256 * u[2]
+                    quantize(0, 0, slice(lo, lo + 256), grp[:, D * g : D * g + D])
 
         def make_cb(s):
             n = s // 8
             k, tl = divmod(s, 4)
-            c_t = cbpool.tile([P, H], F32, name="cb%d" % s, tag="cb")
+            c_t = cbpool.tile([P, D - CUT], F32, name="cb%d" % s, tag="cb")
             nc.gpsimd.tensor_tensor(
-                out=c_t[:], in0=pw_raw[k][:, tl * D + H : (tl + 1) * D], in1=b_all[:, n * D + H : (n + 1) * D], op=ALU.add
+                out=c_t[:], in0=pw_raw[k][:, tl * D + CUT : (tl + 1) * D], in1=b_all[:, n, :], op=ALU.add
             )
             cb_tiles[s] = c_t
 
         def make_c_pe(s):
             n = s // 8
             k, tl = divmod(s, 4)
-            c_ps = psum_c.tile([P, H], F32, name="cps", tag="cps")
-            nc.tensor.matmul(c_ps[:], lhsT=identb[:], rhs=pw_raw[k][:, tl * D : tl * D + H], start=True, stop=False)
-            nc.tensor.matmul(c_ps[:], lhsT=ones[:], rhs=bpad[:, n * D : n * D + H], start=False, stop=True)
+            c_ps = psum_c.tile([P, CUT], F32, name="cps", tag="cps")
+            nc.tensor.matmul(c_ps[:], lhsT=identb[:], rhs=pw_raw[k][:, tl * D : tl * D + CUT], start=True, stop=False)
+            nc.tensor.matmul(c_ps[:], lhsT=sel[:, NB + n, :], rhs=gb[:, 0:CUT], start=False, stop=True)
             cps_tiles[s] = c_ps
 
         def finish_b(s):
             t_t, rstd = state[s]
             nc.vector.scalar_tensor_tensor(
-                out=t_t[:, H:D], in0=t_t[:, H:D], scalar=rstd[:], in1=cb_tiles[s][:], op0=ALU.mult, op1=ALU.add
+                out=t_t[:, CUT:D], in0=t_t[:, CUT:D], scalar=rstd[:], in1=cb_tiles[s][:], op0=ALU.mult, op1=ALU.add
             )
 
         def finish_a(s):
-            n, i = divmod(s, 8)
             t_t, rstd = state[s]
-            c_a = cps_tiles[s] if s in PE_C_SLOTS else ca_tiles[s]
+            c_a = cps_tiles[s]
             nc.vector.scalar_tensor_tensor(
-                out=t_t[:, 0:H], in0=t_t[:, 0:H], scalar=rstd[:], in1=c_a[:], op0=ALU.mult, op1=ALU.add
+                out=t_t[:, 0:CUT], in0=t_t[:, 0:CUT], scalar=rstd[:], in1=c_a[:], op0=ALU.mult, op1=ALU.add
             )
-            nc.sync.dma_start(out=out_view[n][:, i, :], in_=t_t[:])
+
+        def store(s):
+            n, i = divmod(s, 8)
+            nc.sync.dma_start(out=out_view[n][:, i, :], in_=state[s][0][:])
 
         def make_rstd(s):
             t_t, ssq = state[s]
@@ -204,69 +225,59 @@ def tile_moietransformerblock_pb_kernel(tc, in_proto, pt_w, pln_g, pln_b, proto_
             nc.scalar.activation(out=rstd[:], in_=ssq[:], func=ACT.Abs_reciprocal_sqrt, bias=eps[:], scale=1.0 / D)
             state[s] = (t_t, rstd)
 
-        load_chunk(0)
-        load_chunk(1)
-        load_chunk(2)
-        load_pw(0)
-        load_chunk(3)
-        for u in range(HEAD_UNITS):
-            unit_front(u, u % 3)
-            if 0 < u < HEAD_UNITS - 1:
-                unit_back(u - 1)
-            if u >= HEAD_UNITS - 2:
-                unit_back(u)
-            if u == 3:
-                load_pw(1)
+        head = [("w0", 0, q) for q in range(4)] + [("a", 0, 0)]
+        for k, u in enumerate(head):
+            unit_front(u, k % 3, ((1,) if k % 2 == 1 else ()))
+            if k > 0:
+                unit_back(head[k - 1])
+        unit_back(head[-1])
         g_ps = broadcast_g(0)
-        broadcast_b(0, 1)
-        broadcast_b(0, 0)
         make_cb(0)
+        units = prep_units()
         waiting = []
 
         for s in range(N_SLOTS):
             n, i = divmod(s, 8)
-            cd_w, sc_w = codes[(n, 0)]
-            cd_a, sc_a = codes[(n, 1)]
-            rows = slice(P * i, P * i + P)
+            cd_w, sc_w = codes[(0, n)]
+            cd_a, sc_a = codes[(1, n)]
             xs = xsp.tile([P, D], F32, name="xs%d" % s, tag="xs")
             sums = smallp.tile([P, 2], F32, name="sums%d" % s, tag="sums")
             x_ps = []
             for h in range(2):
-                cols = slice(H * h, H * h + H)
                 x_h = psum_x.tile([P, H], F32, name="x", tag="x")
                 for g in range(2):
+                    rows = slice(H * (i // 2) + 256 * g + P * (i % 2), H * (i // 2) + 256 * g + P * (i % 2) + P)
+                    cols = slice(D * g + H * h, D * g + H * h + H)
                     nc.tensor.matmul_mx(
                         out=x_h[:],
-                        lhsT=cd_a[:, g, rows].bitcast(FP8X4),
-                        lhsT_scale=sc_a[:, g, rows],
-                        rhs=cd_w[:, g, cols].bitcast(FP8X4),
-                        rhs_scale=sc_w[:, g, cols],
+                        lhsT=cd_a[:, rows].bitcast(FP8X4),
+                        lhsT_scale=sc_a[:, rows],
+                        rhs=cd_w[:, cols].bitcast(FP8X4),
+                        rhs_scale=sc_w[:, cols],
                         start=(g == 0),
                         stop=(g == 1),
                     )
                 x_ps.append(x_h)
-            if s == 0:
-                for e in EARLY_C_SLOTS:
-                    make_ca(e)
             nc.scalar.activation(out=xs[:, 0:H], in_=x_ps[0][:], func=ACT.Copy, accum_out=sums[:, 0:1])
             if s > 0:
                 make_rstd(s - 1)
             nc.scalar.activation(out=xs[:, H:D], in_=x_ps[1][:], func=ACT.Copy, accum_out=sums[:, 1:2])
-            if s > 0:
-                finish_b(s - 1)
             for u in waiting:
                 unit_back(u)
+            if s > 0:
+                finish_b(s - 1)
+                make_c_pe(s - 1)
+                finish_a(s - 1)
+                store(s - 1)
             if s + 1 < N_SLOTS:
                 make_cb(s + 1)
-                if s + 1 not in PE_C_SLOTS and s + 1 not in EARLY_C_SLOTS:
-                    make_ca(s + 1)
-            if s > 0:
-                if s - 1 in PE_C_SLOTS:
-                    make_c_pe(s - 1)
-                finish_a(s - 1)
-            waiting = units_of_slot(s)
+            waiting = units[0:2] if s == 0 else units[s + 1 : s + 2]
             for k, u in enumerate(waiting):
-                unit_front(u, 2 * k)
+                unit_front(u, 2 * k, (() if (s % 3) == 2 else (1,)))
+                if u[0] == "w" and u[3] == 1 and u[1] == 1:
+                    load_chunk(*((0, 2, 1) if u[2] == 0 else (1, 2, 0)))
+                if u == ("a", 1, 1):
+                    load_chunk(1, 2, 1)
             if s > 0 and i == 0:
                 g_ps = broadcast_g(n)
             negmean = smallp.tile([P, 1], F32, name="nm%d" % s, tag="nm")
@@ -280,12 +291,10 @@ def tile_moietransformerblock_pb_kernel(tc, in_proto, pt_w, pln_g, pln_b, proto_
             ssq = smallp.tile([P, 1], F32, name="ssq%d" % s, tag="ssq")
             nc.scalar.activation(out=junk[:], in_=xs[:], func=ACT.Square, bias=negmean[:], scale=1.0, accum_out=ssq[:])
             state[s] = (t_t, ssq)
-            if s in B_SLOTS:
-                broadcast_b(B_SLOTS[s][0], B_SLOTS[s][1])
-            if s == 1:
-                load_pw(2)
             if s >= 4 and s % 4 == 0 and s // 4 + 2 < 2 * NB:
                 load_pw(s // 4 + 2)
         make_rstd(N_SLOTS - 1)
         finish_b(N_SLOTS - 1)
+        make_c_pe(N_SLOTS - 1)
         finish_a(N_SLOTS - 1)
+        store(N_SLOTS - 1)

@@ -20,7 +20,9 @@ LN_EPS = 1e-5
 FLOPS = 2 * NB * D * D * D
 
 N_SLOTS = 8 * NB
-CUT = 336
+CUT = 288
+
+B_SLOTS = {2: 1, 10: 2}
 
 
 def prep_units():
@@ -101,14 +103,11 @@ def tile_moietransformerblock_pb_kernel(tc, in_proto, pt_w, pln_g, pln_b, proto_
         load_pair(1, 1)
         b_all = const.tile([P, NB, D - CUT], BF16, name="b_all")
         load_pair(1, 2)
-        nc.sync.dma_start(out=b_all[:, 0, :], in_=pln_b[0, CUT:D].partition_broadcast(P))
         load_pw(0)
         load_chunk(0, 1, 0)
         load_pair(1, 3)
         load_chunk(0, 1, 1)
         load_pw(1)
-        for n in range(1, NB):
-            nc.sync.dma_start(out=b_all[:, n, :], in_=pln_b[n, CUT:D].partition_broadcast(P))
         load_chunk(1, 1, 0)
         load_chunk(1, 1, 1)
         load_pw(2)
@@ -126,6 +125,12 @@ def tile_moietransformerblock_pb_kernel(tc, in_proto, pt_w, pln_g, pln_b, proto_
             nc.vector.tensor_copy(out=sel[:, r, :], in_=identb[:, r : r + 1].to_broadcast([P, P]))
         junk = const.tile([P, D], BF16, name="junk")
         junk2 = const.tile([P, 2], F32, name="junk2")
+
+        def broadcast_b(n):
+            for lo, hi in ((CUT, H), (H, D)):
+                ps = psum_t.tile([P, H], F32, name="bc", tag="tr")
+                nc.tensor.matmul(ps[:, 0 : hi - lo], lhsT=sel[:, NB + n, :], rhs=gb[:, lo:hi], start=True, stop=True)
+                nc.scalar.copy(out=b_all[:, n, lo - CUT : hi - CUT], in_=ps[:, 0 : hi - lo])
 
         def broadcast_g(n):
             tiles = []
@@ -232,6 +237,7 @@ def tile_moietransformerblock_pb_kernel(tc, in_proto, pt_w, pln_g, pln_b, proto_
                 unit_back(head[k - 1])
         unit_back(head[-1])
         g_ps = broadcast_g(0)
+        broadcast_b(0)
         make_cb(0)
         units = prep_units()
         waiting = []
@@ -291,6 +297,8 @@ def tile_moietransformerblock_pb_kernel(tc, in_proto, pt_w, pln_g, pln_b, proto_
             ssq = smallp.tile([P, 1], F32, name="ssq%d" % s, tag="ssq")
             nc.scalar.activation(out=junk[:], in_=xs[:], func=ACT.Square, bias=negmean[:], scale=1.0, accum_out=ssq[:])
             state[s] = (t_t, ssq)
+            if s in B_SLOTS:
+                broadcast_b(B_SLOTS[s])
             if s >= 4 and s % 4 == 0 and s // 4 + 2 < 2 * NB:
                 load_pw(s // 4 + 2)
         make_rstd(N_SLOTS - 1)

@@ -20,9 +20,11 @@ LN_EPS = 1e-5
 FLOPS = 2 * NB * D * D * D
 
 N_SLOTS = 8 * NB
-CUT = 288
+CUT = 368
 
-B_SLOTS = {2: 1, 10: 2}
+
+def FOLDS(s):
+    return s % 2 == 1
 
 
 def prep_units():
@@ -52,15 +54,15 @@ def tile_moietransformerblock_pb_kernel(tc, in_proto, pt_w, pln_g, pln_b, proto_
         pwp = ctx.enter_context(tc.tile_pool(name="pwp", bufs=3))
         grpp = ctx.enter_context(tc.tile_pool(name="grpp", bufs=4))
         codep = ctx.enter_context(tc.tile_pool(name="codep", bufs=2))
-        xsp = ctx.enter_context(tc.tile_pool(name="xsp", bufs=3))
+        junkp = ctx.enter_context(tc.tile_pool(name="junkp", bufs=4))
         tpool = ctx.enter_context(tc.tile_pool(name="tpool", bufs=8))
         cbpool = ctx.enter_context(tc.tile_pool(name="cbpool", bufs=2))
         smallp = ctx.enter_context(tc.tile_pool(name="smallp", bufs=4))
         psum_t = ctx.enter_context(tc.psum_pool(name="psum_t", bufs=2))
-        psum_c = ctx.enter_context(tc.psum_pool(name="psum_c", bufs=2))
-        psum_x = ctx.enter_context(tc.psum_pool(name="psum_x", bufs=2))
-        psum_g = ctx.enter_context(tc.psum_pool(name="psum_g", bufs=2))
-        tr_homes = ((psum_t, "tr"), (psum_x, "x"), (psum_c, "cps"))
+        psum_c = ctx.enter_context(tc.psum_pool(name="psum_c", bufs=1))
+        psum_x = ctx.enter_context(tc.psum_pool(name="psum_x", bufs=4))
+        psum_s = ctx.enter_context(tc.psum_pool(name="psum_s", bufs=1))
+        tr_homes = ((psum_t, "tr"), (psum_x, "x"), (psum_x, "x"))
 
         raw = {}
         pw_raw = {}
@@ -69,6 +71,9 @@ def tile_moietransformerblock_pb_kernel(tc, in_proto, pt_w, pln_g, pln_b, proto_
         cps_tiles = {}
         state = {}
         unit = {}
+        turned = {}
+        x_tiles = {}
+        negmeans = {}
 
         def load_pair(op, q):
             view = w_view if op == 0 else a_view
@@ -123,22 +128,22 @@ def tile_moietransformerblock_pb_kernel(tc, in_proto, pt_w, pln_g, pln_b, proto_
         sel = const.tile([P, 2 * NB, P], BF16, name="sel")
         for r in range(2 * NB):
             nc.vector.tensor_copy(out=sel[:, r, :], in_=identb[:, r : r + 1].to_broadcast([P, P]))
-        junk = const.tile([P, D], BF16, name="junk")
+        g_all = const.tile([P, NB, D], BF16, name="g_all")
         junk2 = const.tile([P, 2], F32, name="junk2")
 
-        def broadcast_b(n):
-            for lo, hi in ((CUT, H), (H, D)):
-                ps = psum_t.tile([P, H], F32, name="bc", tag="tr")
-                nc.tensor.matmul(ps[:, 0 : hi - lo], lhsT=sel[:, NB + n, :], rhs=gb[:, lo:hi], start=True, stop=True)
-                nc.scalar.copy(out=b_all[:, n, lo - CUT : hi - CUT], in_=ps[:, 0 : hi - lo])
+        def spread_first():
+            for k, (row, lo, hi) in enumerate(((0, 0, H), (0, H, D), (NB, CUT, H), (NB, H, D))):
+                ps = psum_x.tile([P, H], F32, name="bc", tag="x")
+                nc.tensor.matmul(ps[:, 0 : hi - lo], lhsT=sel[:, row, :], rhs=gb[:, lo:hi], start=True, stop=True)
+                dst = g_all[:, 0, lo:hi] if row == 0 else b_all[:, 0, lo - CUT : hi - CUT]
+                if k % 2 == 0:
+                    nc.scalar.copy(out=dst, in_=ps[:, 0 : hi - lo])
+                else:
+                    nc.vector.tensor_copy(out=dst, in_=ps[:, 0 : hi - lo])
 
-        def broadcast_g(n):
-            tiles = []
-            for h in range(2):
-                g_h = psum_g.tile([P, H], F32, name="gps", tag="gps")
-                nc.tensor.matmul(g_h[:], lhsT=sel[:, n, :], rhs=gb[:, H * h : H * h + H], start=True, stop=True)
-                tiles.append(g_h)
-            return tiles
+        def spread(n):
+            nc.sync.dma_start(out=g_all[:, n, :], in_=pln_g[n, :].partition_broadcast(P))
+            nc.sync.dma_start(out=b_all[:, n, :], in_=pln_b[n, CUT:D].partition_broadcast(P))
 
         def code_tiles(op, n):
             if (op, n) not in codes:
@@ -147,8 +152,7 @@ def tile_moietransformerblock_pb_kernel(tc, in_proto, pt_w, pln_g, pln_b, proto_
                 codes[(op, n)] = (cd, sc)
             return codes[(op, n)]
 
-        def unit_front(u, home, v_copies):
-            pool, tag = tr_homes[home]
+        def unit_source(u):
             if u[0] == "w":
                 words = raw[(0, u[1], u[2])][:].bitcast(F32)
                 starts = [[H * (2 * h + tl) + 256 * u[3] for tl in range(2)] for h in range(2)]
@@ -158,21 +162,32 @@ def tile_moietransformerblock_pb_kernel(tc, in_proto, pt_w, pln_g, pln_b, proto_
             else:
                 words = raw[("h", 0 if u[0] == "w0" else 1, u[2])][:].bitcast(F32)
                 starts = [[H * tl + 256 * h for tl in range(2)] for h in range(2)]
-            grp = grpp.tile([P, 2048], BF16, name="grp", tag="grp", align_bytes=64)
-            grp_w = grp[:].bitcast(F32).rearrange("p (a r w) -> p a r w", a=4, w=2)
+            return words, starts
+
+        def turn(u, h, home):
+            pool, tag = tr_homes[home]
+            words, starts = unit_source(u)
+            if h == 0:
+                unit[u] = grpp.tile([P, 2048], BF16, name="grp", tag="grp", align_bytes=64)
+            ps = pool.tile([P, 2, 2, P], F32, name="tr", tag=tag)
+            for tl in range(2):
+                for w in range(2):
+                    col = starts[h][tl]
+                    nc.tensor.transpose(ps[:, tl, w, :], words[:, col + w : col + 256 : 2], ident[:])
+            turned[(u, h)] = ps
+
+        def gather(u, h, on_vector):
+            src = turned[(u, h)][:].rearrange("p a w r -> p a r w")
+            dst = unit[u][:].bitcast(F32).rearrange("p (a r w) -> p a r w", a=4, w=2)[:, 2 * h : 2 * h + 2]
+            if on_vector:
+                nc.vector.tensor_copy(out=dst, in_=src)
+            else:
+                nc.scalar.copy(out=dst, in_=src)
+
+        def unit_front(u, home, v_copies):
             for h in range(2):
-                ps = pool.tile([P, 2, 2, P], F32, name="tr", tag=tag)
-                for tl in range(2):
-                    for w in range(2):
-                        col = starts[h][tl]
-                        nc.tensor.transpose(ps[:, tl, w, :], words[:, col + w : col + 256 : 2], ident[:])
-                src = ps[:].rearrange("p a w r -> p a r w")
-                dst = grp_w[:, 2 * h : 2 * h + 2]
-                if h in v_copies:
-                    nc.vector.tensor_copy(out=dst, in_=src)
-                else:
-                    nc.scalar.copy(out=dst, in_=src)
-            unit[u] = grp
+                turn(u, h, home)
+                gather(u, h, h in v_copies)
 
         def quantize(op, n, cols, in_):
             cd, sc = code_tiles(op, n)
@@ -224,11 +239,83 @@ def tile_moietransformerblock_pb_kernel(tc, in_proto, pt_w, pln_g, pln_b, proto_
             n, i = divmod(s, 8)
             nc.sync.dma_start(out=out_view[n][:, i, :], in_=state[s][0][:])
 
-        def make_rstd(s):
-            t_t, ssq = state[s]
+        def mx(out, s, cols, g):
+            n, i = divmod(s, 8)
+            cd_w, sc_w = codes[(0, n)]
+            cd_a, sc_a = codes[(1, n)]
+            lo = H * (i // 2) + 256 * g + P * (i % 2)
+            rows = slice(lo, lo + P)
+            return dict(
+                out=out,
+                lhsT=cd_a[:, rows].bitcast(FP8X4),
+                lhsT_scale=sc_a[:, rows],
+                rhs=cd_w[:, cols].bitcast(FP8X4),
+                rhs_scale=sc_w[:, cols],
+            )
+
+        def fold(s):
+            f_ps = psum_s.tile([P, P], F32, name="f", tag="f")
+            for g in range(2):
+                for j in range(8):
+                    cols = slice(D * g + P * j, D * g + P * j + P)
+                    nc.tensor.matmul_mx(**mx(f_ps[:], s, cols, g), start=(g == 0 and j == 0), stop=(g == 1 and j == 7))
+            x_tiles[(s, "f")] = f_ps
+
+        def multiply(s, h):
+            x_h = psum_x.tile([P, H], F32, name="x", tag="x")
+            for g in range(2):
+                cols = slice(D * g + H * h, D * g + H * h + H)
+                nc.tensor.matmul_mx(**mx(x_h[:], s, cols, g), start=(g == 0), stop=(g == 1))
+            x_tiles[(s, h)] = x_h
+
+        def product(s):
+            if FOLDS(s):
+                fold(s)
+            multiply(s, 0)
+            multiply(s, 1)
+
+        def take_mean(s):
+            negmean = smallp.tile([P, 1], F32, name="nm%d" % s, tag="nm")
+            if FOLDS(s):
+                junk = junkp.tile([P, H], BF16, name="junk", tag="junk")
+                nc.scalar.activation(
+                    out=junk[:, 0:P], in_=x_tiles[(s, "f")][:], func=ACT.Copy, scale=-1.0 / D, accum_out=negmean[:]
+                )
+            else:
+                sums = smallp.tile([P, 2], F32, name="sums%d" % s, tag="sums")
+                for h in range(2):
+                    junk = junkp.tile([P, H], BF16, name="junk", tag="junk")
+                    nc.scalar.activation(out=junk[:], in_=x_tiles[(s, h)][:], func=ACT.Copy, accum_out=sums[:, h : h + 1])
+                nc.scalar.activation(out=junk2[:], in_=sums[:], func=ACT.Copy, scale=-1.0 / D, accum_out=negmean[:])
+            negmeans[s] = negmean
+
+        def take_squares(s):
+            out = []
+            for h in range(2):
+                junk = junkp.tile([P, H], BF16, name="junk", tag="junk")
+                ssq = smallp.tile([P, 1], F32, name="ssq%d_%d" % (s, h), tag="ssq%d" % h)
+                nc.scalar.activation(
+                    out=junk[:], in_=x_tiles[(s, h)][:], func=ACT.Square, bias=negmeans[s][:], scale=1.0, accum_out=ssq[:]
+                )
+                out.append(ssq)
+            part = smallp.tile([P, 1], F32, name="part%d" % s, tag="part")
+            nc.scalar.activation(out=part[:], in_=out[0][:], func=ACT.Identity, bias=eps[:], scale=1.0 / D)
+            return part, out[1]
+
+        def make_rstd(s, part, ssq):
             rstd = smallp.tile([P, 1], F32, name="rstd%d" % s, tag="rstd")
-            nc.scalar.activation(out=rstd[:], in_=ssq[:], func=ACT.Abs_reciprocal_sqrt, bias=eps[:], scale=1.0 / D)
-            state[s] = (t_t, rstd)
+            nc.scalar.activation(out=rstd[:], in_=ssq[:], func=ACT.Abs_reciprocal_sqrt, bias=part[:], scale=1.0 / D)
+            return rstd
+
+        def scale_g(s):
+            t_t = tpool.tile([P, D], F32, name="t%d" % s, tag="t")
+            for h in range(2):
+                cols = slice(H * h, H * h + H)
+                nc.vector.scalar_tensor_tensor(
+                    out=t_t[:, cols], in0=x_tiles[(s, h)][:], scalar=negmeans[s][:], in1=g_all[:, s // 8, cols],
+                    op0=ALU.add, op1=ALU.mult,
+                )
+            return t_t
 
         head = [("w0", 0, q) for q in range(4)] + [("a", 0, 0)]
         for k, u in enumerate(head):
@@ -236,38 +323,25 @@ def tile_moietransformerblock_pb_kernel(tc, in_proto, pt_w, pln_g, pln_b, proto_
             if k > 0:
                 unit_back(head[k - 1])
         unit_back(head[-1])
-        g_ps = broadcast_g(0)
-        broadcast_b(0)
+        spread_first()
+        product(0)
         make_cb(0)
         units = prep_units()
-        waiting = []
+        for h in range(2):
+            turn(units[0], h, 0)
+            gather(units[0], h, True)
+        waiting = units[0:1]
 
         for s in range(N_SLOTS):
             n, i = divmod(s, 8)
-            cd_w, sc_w = codes[(0, n)]
-            cd_a, sc_a = codes[(1, n)]
-            xs = xsp.tile([P, D], F32, name="xs%d" % s, tag="xs")
-            sums = smallp.tile([P, 2], F32, name="sums%d" % s, tag="sums")
-            x_ps = []
-            for h in range(2):
-                x_h = psum_x.tile([P, H], F32, name="x", tag="x")
-                for g in range(2):
-                    rows = slice(H * (i // 2) + 256 * g + P * (i % 2), H * (i // 2) + 256 * g + P * (i % 2) + P)
-                    cols = slice(D * g + H * h, D * g + H * h + H)
-                    nc.tensor.matmul_mx(
-                        out=x_h[:],
-                        lhsT=cd_a[:, rows].bitcast(FP8X4),
-                        lhsT_scale=sc_a[:, rows],
-                        rhs=cd_w[:, cols].bitcast(FP8X4),
-                        rhs_scale=sc_w[:, cols],
-                        start=(g == 0),
-                        stop=(g == 1),
-                    )
-                x_ps.append(x_h)
-            nc.scalar.activation(out=xs[:, 0:H], in_=x_ps[0][:], func=ACT.Copy, accum_out=sums[:, 0:1])
-            if s > 0:
-                make_rstd(s - 1)
-            nc.scalar.activation(out=xs[:, H:D], in_=x_ps[1][:], func=ACT.Copy, accum_out=sums[:, 1:2])
+            last = s + 1 == N_SLOTS
+            new_units = units[s + 1 : s + 2]
+            v_copies = ((1,) if s % 3 == 0 else ())
+            for u in new_units:
+                turn(u, 0, 0)
+                turn(u, 1, 0)
+            take_mean(s)
+            part, ssq = take_squares(s)
             for u in waiting:
                 unit_back(u)
             if s > 0:
@@ -275,33 +349,23 @@ def tile_moietransformerblock_pb_kernel(tc, in_proto, pt_w, pln_g, pln_b, proto_
                 make_c_pe(s - 1)
                 finish_a(s - 1)
                 store(s - 1)
-            if s + 1 < N_SLOTS:
+            if not last:
                 make_cb(s + 1)
-            waiting = units[0:2] if s == 0 else units[s + 1 : s + 2]
-            for k, u in enumerate(waiting):
-                unit_front(u, 2 * k, (() if (s % 3) == 2 else (1,)))
+            for u in new_units:
+                gather(u, 0, 0 in v_copies)
+                gather(u, 1, 1 in v_copies)
                 if u[0] == "w" and u[3] == 1 and u[1] == 1:
                     load_chunk(*((0, 2, 1) if u[2] == 0 else (1, 2, 0)))
                 if u == ("a", 1, 1):
                     load_chunk(1, 2, 1)
-            if s > 0 and i == 0:
-                g_ps = broadcast_g(n)
-            negmean = smallp.tile([P, 1], F32, name="nm%d" % s, tag="nm")
-            nc.scalar.activation(out=junk2[:], in_=sums[:], func=ACT.Copy, scale=-1.0 / D, accum_out=negmean[:])
-            t_t = tpool.tile([P, D], F32, name="t%d" % s, tag="t")
-            for h in (1, 0):
-                cols = slice(H * h, H * h + H)
-                nc.vector.scalar_tensor_tensor(
-                    out=t_t[:, cols], in0=xs[:, cols], scalar=negmean[:], in1=g_ps[h][:], op0=ALU.add, op1=ALU.mult
-                )
-            ssq = smallp.tile([P, 1], F32, name="ssq%d" % s, tag="ssq")
-            nc.scalar.activation(out=junk[:], in_=xs[:], func=ACT.Square, bias=negmean[:], scale=1.0, accum_out=ssq[:])
-            state[s] = (t_t, ssq)
-            if s in B_SLOTS:
-                broadcast_b(B_SLOTS[s])
+            state[s] = (scale_g(s), make_rstd(s, part, ssq))
+            if not last:
+                product(s + 1)
+            waiting = new_units
+            if s in (1, 8):
+                spread(1 if s == 1 else 2)
             if s >= 4 and s % 4 == 0 and s // 4 + 2 < 2 * NB:
                 load_pw(s // 4 + 2)
-        make_rstd(N_SLOTS - 1)
         finish_b(N_SLOTS - 1)
         make_c_pe(N_SLOTS - 1)
         finish_a(N_SLOTS - 1)

@@ -24,7 +24,7 @@ CUT = 368
 
 
 def FOLDS(s):
-    return s % 2 == 1
+    return s % 2 == 1 and s > 2
 
 
 def prep_units():
@@ -62,7 +62,7 @@ def tile_moietransformerblock_pb_kernel(tc, in_proto, pt_w, pln_g, pln_b, proto_
         psum_c = ctx.enter_context(tc.psum_pool(name="psum_c", bufs=1))
         psum_x = ctx.enter_context(tc.psum_pool(name="psum_x", bufs=4))
         psum_s = ctx.enter_context(tc.psum_pool(name="psum_s", bufs=1))
-        tr_homes = ((psum_t, "tr"), (psum_x, "x"), (psum_x, "x"))
+        tr_homes = ((psum_t, "tr"), (psum_x, "x"), (psum_x, "x"), (psum_s, "f"), (psum_c, "cps"))
 
         raw = {}
         pw_raw = {}
@@ -235,6 +235,11 @@ def tile_moietransformerblock_pb_kernel(tc, in_proto, pt_w, pln_g, pln_b, proto_
                 out=t_t[:, 0:CUT], in0=t_t[:, 0:CUT], scalar=rstd[:], in1=c_a[:], op0=ALU.mult, op1=ALU.add
             )
 
+        def finish(s, wide_first):
+            parts = (finish_b, finish_a) if wide_first else (finish_a, finish_b)
+            for part in parts:
+                part(s)
+
         def store(s):
             n, i = divmod(s, 8)
             nc.sync.dma_start(out=out_view[n][:, i, :], in_=state[s][0][:])
@@ -325,48 +330,56 @@ def tile_moietransformerblock_pb_kernel(tc, in_proto, pt_w, pln_g, pln_b, proto_
         unit_back(head[-1])
         spread_first()
         product(0)
+        product(1)
         make_cb(0)
         units = prep_units()
         for h in range(2):
             turn(units[0], h, 0)
-            gather(units[0], h, True)
-        waiting = units[0:1]
+        waiting = []
 
         for s in range(N_SLOTS):
             n, i = divmod(s, 8)
             last = s + 1 == N_SLOTS
-            new_units = units[s + 1 : s + 2]
-            v_copies = ((1,) if s % 3 == 0 else ())
+            new_units = units[0:2] if s == 0 else units[s + 1 : s + 2]
+            v_copies = ((1,) if s % 3 == 1 else ())
             for u in new_units:
-                turn(u, 0, 0)
-                turn(u, 1, 0)
+                if u != units[0]:
+                    for h in range(2):
+                        turn(u, h, 3 + h if s == 0 else 0)
             take_mean(s)
             part, ssq = take_squares(s)
             for u in waiting:
                 unit_back(u)
             if s > 0:
-                finish_b(s - 1)
                 make_c_pe(s - 1)
-                finish_a(s - 1)
+                finish(s - 1, bool(waiting))
                 store(s - 1)
             if not last:
                 make_cb(s + 1)
+            if s > 0:
+                for u in new_units:
+                    gather(u, 0, 0 in v_copies)
+                    gather(u, 1, 1 in v_copies)
             for u in new_units:
-                gather(u, 0, 0 in v_copies)
-                gather(u, 1, 1 in v_copies)
                 if u[0] == "w" and u[3] == 1 and u[1] == 1:
                     load_chunk(*((0, 2, 1) if u[2] == 0 else (1, 2, 0)))
                 if u == ("a", 1, 1):
                     load_chunk(1, 2, 1)
-            state[s] = (scale_g(s), make_rstd(s, part, ssq))
-            if not last:
+            t_t = scale_g(s)
+            if s == 0:
+                for u in new_units:
+                    gather(u, 0, u == units[0])
+                    gather(u, 1, True)
+            state[s] = (t_t, make_rstd(s, part, ssq))
+            if s > 0 and not last:
                 product(s + 1)
             waiting = new_units
             if s in (1, 8):
                 spread(1 if s == 1 else 2)
             if s >= 4 and s % 4 == 0 and s // 4 + 2 < 2 * NB:
                 load_pw(s // 4 + 2)
-        finish_b(N_SLOTS - 1)
         make_c_pe(N_SLOTS - 1)
         finish_a(N_SLOTS - 1)
-        store(N_SLOTS - 1)
+        nc.sync.dma_start(out=out_view[NB - 1][:, 7, 0:CUT], in_=state[N_SLOTS - 1][0][:, 0:CUT])
+        finish_b(N_SLOTS - 1)
+        nc.sync.dma_start(out=out_view[NB - 1][:, 7, CUT:D], in_=state[N_SLOTS - 1][0][:, CUT:D])

@@ -74,6 +74,7 @@ def tile_moietransformerblock_pb_kernel(tc, in_proto, pt_w, pln_g, pln_b, proto_
         turned = {}
         x_tiles = {}
         negmeans = {}
+        all_sums = {}
 
         def load_pair(op, q):
             view = w_view if op == 0 else a_view
@@ -131,15 +132,14 @@ def tile_moietransformerblock_pb_kernel(tc, in_proto, pt_w, pln_g, pln_b, proto_
         g_all = const.tile([P, NB, D], BF16, name="g_all")
         junk2 = const.tile([P, 2], F32, name="junk2")
 
-        def spread_first():
-            for k, (row, lo, hi) in enumerate(((0, 0, H), (0, H, D), (NB, CUT, H), (NB, H, D))):
-                ps = psum_x.tile([P, H], F32, name="bc", tag="x")
-                nc.tensor.matmul(ps[:, 0 : hi - lo], lhsT=sel[:, row, :], rhs=gb[:, lo:hi], start=True, stop=True)
-                dst = g_all[:, 0, lo:hi] if row == 0 else b_all[:, 0, lo - CUT : hi - CUT]
-                if k % 2 == 0:
-                    nc.scalar.copy(out=dst, in_=ps[:, 0 : hi - lo])
-                else:
-                    nc.vector.tensor_copy(out=dst, in_=ps[:, 0 : hi - lo])
+        def spread_first(row, lo, hi, pool, tag, on_vector):
+            ps = pool.tile([P, H], F32, name="bc", tag=tag)
+            nc.tensor.matmul(ps[:, 0 : hi - lo], lhsT=sel[:, row, :], rhs=gb[:, lo:hi], start=True, stop=True)
+            dst = g_all[:, 0, lo:hi] if row == 0 else b_all[:, 0, lo - CUT : hi - CUT]
+            if on_vector:
+                nc.vector.tensor_copy(out=dst, in_=ps[:, 0 : hi - lo])
+            else:
+                nc.scalar.copy(out=dst, in_=ps[:, 0 : hi - lo])
 
         def spread(n):
             nc.sync.dma_start(out=g_all[:, n, :], in_=pln_g[n, :].partition_broadcast(P))
@@ -158,10 +158,12 @@ def tile_moietransformerblock_pb_kernel(tc, in_proto, pt_w, pln_g, pln_b, proto_
                 starts = [[H * (2 * h + tl) + 256 * u[3] for tl in range(2)] for h in range(2)]
             elif u[0] == "a" and u[1] > 0:
                 words = raw[(1, u[1], u[2] // 2)][:].bitcast(F32)
-                starts = [[H * (2 * (u[2] % 2) + tl) + 256 * h for tl in range(2)] for h in range(2)]
+                starts = [[H * (2 * (u[2] % 2) + h) + 256 * g for g in range(2)] for h in range(2)]
             else:
                 words = raw[("h", 0 if u[0] == "w0" else 1, u[2])][:].bitcast(F32)
-                starts = [[H * tl + 256 * h for tl in range(2)] for h in range(2)]
+                starts = [[H * tl + 256 * g for tl in range(2)] for g in range(2)]
+                if u[0] == "a":
+                    starts = [[H * tl + 256 * g for g in range(2)] for tl in range(2)]
             return words, starts
 
         def turn(u, h, home):
@@ -248,7 +250,7 @@ def tile_moietransformerblock_pb_kernel(tc, in_proto, pt_w, pln_g, pln_b, proto_
             n, i = divmod(s, 8)
             cd_w, sc_w = codes[(0, n)]
             cd_a, sc_a = codes[(1, n)]
-            lo = H * (i // 2) + 256 * g + P * (i % 2)
+            lo = H * (i // 2) + 256 * (i % 2) + P * g
             rows = slice(lo, lo + P)
             return dict(
                 out=out,
@@ -279,6 +281,15 @@ def tile_moietransformerblock_pb_kernel(tc, in_proto, pt_w, pln_g, pln_b, proto_
             multiply(s, 0)
             multiply(s, 1)
 
+        def take_sums(s):
+            if FOLDS(s):
+                return
+            sums = smallp.tile([P, 2], F32, name="sums%d" % s, tag="sums")
+            for h in range(2):
+                junk = junkp.tile([P, H], BF16, name="junk", tag="junk")
+                nc.scalar.activation(out=junk[:], in_=x_tiles[(s, h)][:], func=ACT.Copy, accum_out=sums[:, h : h + 1])
+            all_sums[s] = sums
+
         def take_mean(s):
             negmean = smallp.tile([P, 1], F32, name="nm%d" % s, tag="nm")
             if FOLDS(s):
@@ -287,11 +298,9 @@ def tile_moietransformerblock_pb_kernel(tc, in_proto, pt_w, pln_g, pln_b, proto_
                     out=junk[:, 0:P], in_=x_tiles[(s, "f")][:], func=ACT.Copy, scale=-1.0 / D, accum_out=negmean[:]
                 )
             else:
-                sums = smallp.tile([P, 2], F32, name="sums%d" % s, tag="sums")
-                for h in range(2):
-                    junk = junkp.tile([P, H], BF16, name="junk", tag="junk")
-                    nc.scalar.activation(out=junk[:], in_=x_tiles[(s, h)][:], func=ACT.Copy, accum_out=sums[:, h : h + 1])
-                nc.scalar.activation(out=junk2[:], in_=sums[:], func=ACT.Copy, scale=-1.0 / D, accum_out=negmean[:])
+                nc.scalar.activation(
+                    out=junk2[:], in_=all_sums[s][:], func=ACT.Copy, scale=-1.0 / D, accum_out=negmean[:]
+                )
             negmeans[s] = negmean
 
         def take_squares(s):
@@ -322,13 +331,23 @@ def tile_moietransformerblock_pb_kernel(tc, in_proto, pt_w, pln_g, pln_b, proto_
                 )
             return t_t
 
-        head = [("w0", 0, q) for q in range(4)] + [("a", 0, 0)]
+        head = [("w0", 0, q) for q in range(4)]
+        first = ("a", 0, 0)
         for k, u in enumerate(head):
-            unit_front(u, k % 3, ((1,) if k % 2 == 1 else ()))
+            unit_front(u, k % 3, ((1,) if k == 1 else ()))
             if k > 0:
                 unit_back(head[k - 1])
+        turn(first, 0, 1)
+        gather(first, 0, False)
         unit_back(head[-1])
-        spread_first()
+        quantize(1, 0, slice(0, 256), unit[first][:, 0:D])
+        turn(first, 1, 1)
+        gather(first, 1, False)
+        for lo in (0, H):
+            spread_first(0, lo, lo + H, psum_x, "x", lo == 0)
+        spread_first(NB, CUT, H, psum_s, "f", False)
+        spread_first(NB, H, D, psum_c, "cps", True)
+        quantize(1, 0, slice(256, H), unit[first][:, D : 2 * D])
         product(0)
         product(1)
         make_cb(0)
@@ -346,6 +365,10 @@ def tile_moietransformerblock_pb_kernel(tc, in_proto, pt_w, pln_g, pln_b, proto_
                 if u != units[0]:
                     for h in range(2):
                         turn(u, h, 3 + h if s == 0 else 0)
+            take_sums(s)
+            if s > 0 and not FOLDS(s):
+                for u in new_units:
+                    gather(u, 0, 0 in v_copies)
             take_mean(s)
             part, ssq = take_squares(s)
             for u in waiting:
@@ -358,7 +381,8 @@ def tile_moietransformerblock_pb_kernel(tc, in_proto, pt_w, pln_g, pln_b, proto_
                 make_cb(s + 1)
             if s > 0:
                 for u in new_units:
-                    gather(u, 0, 0 in v_copies)
+                    if FOLDS(s):
+                        gather(u, 0, 0 in v_copies)
                     gather(u, 1, 1 in v_copies)
             for u in new_units:
                 if u[0] == "w" and u[3] == 1 and u[1] == 1:

@@ -281,13 +281,20 @@ def tile_moietransformerblock_pb_kernel(tc, in_proto, pt_w, pln_g, pln_b, proto_
             multiply(s, 0)
             multiply(s, 1)
 
-        def take_sums(s):
+        def settle(due):
+            if due is not None:
+                s, part, ssq = due
+                state[s] = (state[s][0], make_rstd(s, part, ssq))
+
+        def take_sums(s, due):
             if FOLDS(s):
                 return
             sums = smallp.tile([P, 2], F32, name="sums%d" % s, tag="sums")
             for h in range(2):
                 junk = junkp.tile([P, H], BF16, name="junk", tag="junk")
                 nc.scalar.activation(out=junk[:], in_=x_tiles[(s, h)][:], func=ACT.Copy, accum_out=sums[:, h : h + 1])
+                if h == 0:
+                    settle(due)
             all_sums[s] = sums
 
         def take_mean(s):
@@ -356,6 +363,7 @@ def tile_moietransformerblock_pb_kernel(tc, in_proto, pt_w, pln_g, pln_b, proto_
             turn(units[0], h, 0)
         waiting = []
 
+        due = None
         for s in range(N_SLOTS):
             n, i = divmod(s, 8)
             last = s + 1 == N_SLOTS
@@ -365,11 +373,13 @@ def tile_moietransformerblock_pb_kernel(tc, in_proto, pt_w, pln_g, pln_b, proto_
                 if u != units[0]:
                     for h in range(2):
                         turn(u, h, 3 + h if s == 0 else 0)
-            take_sums(s)
+            take_sums(s, due)
             if s > 0 and not FOLDS(s):
                 for u in new_units:
                     gather(u, 0, 0 in v_copies)
             take_mean(s)
+            if FOLDS(s):
+                settle(due)
             part, ssq = take_squares(s)
             for u in waiting:
                 unit_back(u)
@@ -394,7 +404,8 @@ def tile_moietransformerblock_pb_kernel(tc, in_proto, pt_w, pln_g, pln_b, proto_
                 for u in new_units:
                     gather(u, 0, u == units[0])
                     gather(u, 1, True)
-            state[s] = (t_t, make_rstd(s, part, ssq))
+            state[s] = (t_t, None)
+            due = (s, part, ssq)
             if s > 0 and not last:
                 product(s + 1)
             waiting = new_units
@@ -402,6 +413,7 @@ def tile_moietransformerblock_pb_kernel(tc, in_proto, pt_w, pln_g, pln_b, proto_
                 spread(1 if s == 1 else 2)
             if s >= 4 and s % 4 == 0 and s // 4 + 2 < 2 * NB:
                 load_pw(s // 4 + 2)
+        settle(due)
         make_c_pe(N_SLOTS - 1)
         finish_a(N_SLOTS - 1)
         nc.sync.dma_start(out=out_view[NB - 1][:, 7, 0:CUT], in_=state[N_SLOTS - 1][0][:, 0:CUT])

@@ -56,7 +56,7 @@ def tile_moietransformerblock_pb_kernel(tc, in_proto, pt_w, pln_g, pln_b, proto_
         codep = ctx.enter_context(tc.tile_pool(name="codep", bufs=2))
         junkp = ctx.enter_context(tc.tile_pool(name="junkp", bufs=4))
         tpool = ctx.enter_context(tc.tile_pool(name="tpool", bufs=8))
-        cbpool = ctx.enter_context(tc.tile_pool(name="cbpool", bufs=2))
+        cbpool = ctx.enter_context(tc.tile_pool(name="cbpool", bufs=3))
         smallp = ctx.enter_context(tc.tile_pool(name="smallp", bufs=4))
         psum_t = ctx.enter_context(tc.psum_pool(name="psum_t", bufs=2))
         psum_c = ctx.enter_context(tc.psum_pool(name="psum_c", bufs=1))
@@ -368,7 +368,7 @@ def tile_moietransformerblock_pb_kernel(tc, in_proto, pt_w, pln_g, pln_b, proto_
             n, i = divmod(s, 8)
             last = s + 1 == N_SLOTS
             new_units = units[0:2] if s == 0 else units[s + 1 : s + 2]
-            v_copies = ((1,) if s % 3 == 1 else ())
+            v_copies = ((1,) if s % 6 == 1 else ())
             for u in new_units:
                 if u != units[0]:
                     for h in range(2):

from contextlib import ExitStack

import concourse.mybir as mybir
from concourse.masks import make_identity

F32 = mybir.dt.float32
BF16 = mybir.dt.bfloat16
U32 = mybir.dt.uint32
U8 = mybir.dt.uint8
I32 = mybir.dt.int32
FP8X4 = mybir.dt.float8_e4m3fn_x4
ACT = mybir.ActivationFunctionType
ALU = mybir.AluOpType

NB = 3
D = 1024
P = 128
H = 512
LN_EPS = 1e-5
FLOPS = 2 * NB * D * D * D

N_SLOTS = 8 * NB
CUT = 368


def FOLDS(s):
    return s % 2 == 1 and s > 2


def prep_units():
    units = []
    for n in range(NB):
        a = [("a", n, q) for q in (1, 2, 3)]
        if n + 1 < NB:
            w = [("w", n + 1, j, g) for j in range(2) for g in range(2)]
            units += [a[0], a[1], w[0], w[1], a[2], w[2], w[3], ("a", n + 1, 0)]
        else:
            units += a
    return units


def tile_moietransformerblock_pb_kernel(tc, in_proto, pt_w, pln_g, pln_b, proto_w, out):
    nc = tc.nc
    a_view = in_proto.rearrange("n (p t) k -> n p t k", t=8)
    w_view = pt_w.rearrange("n (t p) k -> n p t k", p=P)
    pw_view = proto_w.rearrange("n (p t) d -> n p t d", t=8)
    out_view = out.rearrange("n (p t) d -> n p t d", t=8)

    with ExitStack() as ctx:
        ctx.enter_context(tc.manual_schedule())
        const = ctx.enter_context(tc.tile_pool(name="const", bufs=1))
        headp = ctx.enter_context(tc.tile_pool(name="headp", bufs=8))
        rawp = ctx.enter_context(tc.tile_pool(name="rawp", bufs=5))
        pwp = ctx.enter_context(tc.tile_pool(name="pwp", bufs=3))
        grpp = ctx.enter_context(tc.tile_pool(name="grpp", bufs=4))
        codep = ctx.enter_context(tc.tile_pool(name="codep", bufs=2))
        junkp = ctx.enter_context(tc.tile_pool(name="junkp", bufs=4))
        tpool = ctx.enter_context(tc.tile_pool(name="tpool", bufs=8))
        cbpool = ctx.enter_context(tc.tile_pool(name="cbpool", bufs=3))
        smallp = ctx.enter_context(tc.tile_pool(name="smallp", bufs=4))
        psum_t = ctx.enter_context(tc.psum_pool(name="psum_t", bufs=2))
        psum_c = ctx.enter_context(tc.psum_pool(name="psum_c", bufs=1))
        psum_x = ctx.enter_context(tc.psum_pool(name="psum_x", bufs=4))
        psum_s = ctx.enter_context(tc.psum_pool(name="psum_s", bufs=1))
        tr_homes = ((psum_t, "tr"), (psum_x, "x"), (psum_x, "x"), (psum_s, "f"), (psum_c, "cps"))

        raw = {}
        pw_raw = {}
        codes = {}
        cb_tiles = {}
        cps_tiles = {}
        state = {}
        unit = {}
        turned = {}
        x_tiles = {}
        negmeans = {}
        all_sums = {}

        def load_pair(op, q):
            view = w_view if op == 0 else a_view
            t_raw = headp.tile([P, 2 * D], BF16, name="h%d_%d" % (op, q), tag="h")
            nc.sync.dma_start(out=t_raw[:].rearrange("p (t k) -> p t k", t=2), in_=view[0][:, 2 * q : 2 * q + 2, :])
            raw[("h", op, q)] = t_raw

        def load_chunk(op, n, j):
            view = w_view if op == 0 else a_view
            t_raw = rawp.tile([P, 4 * D], BF16, name="raw%d_%d_%d" % (op, n, j), tag="raw")
            nc.sync.dma_start(out=t_raw[:].rearrange("p (t k) -> p t k", t=4), in_=view[n][:, 4 * j : 4 * j + 4, :])
            raw[(op, n, j)] = t_raw

        def load_pw(k):
            n, j = divmod(k, 2)
            t_pw = pwp.tile([P, 4 * D], BF16, name="pw%d" % k, tag="pw")
            nc.sync.dma_start(
                out=t_pw[:].rearrange("p (t k) -> p t k", t=4),
                in_=pw_view[n][:, 4 * j : 4 * j + 4, :],
            )
            pw_raw[k] = t_pw

        load_pair(0, 0)
        load_pair(0, 1)
        gb = const.tile([P, D], BF16, name="gb")
        nc.vector.memset(gb[:].bitcast(I32), 0)
        nc.sync.dma_start(out=gb[0:NB, :], in_=pln_g)
        nc.sync.dma_start(out=gb[NB : 2 * NB, :], in_=pln_b)
        load_pair(0, 2)
        load_pair(0, 3)
        load_pair(1, 0)
        load_pair(1, 1)
        b_all = const.tile([P, NB, D - CUT], BF16, name="b_all")
        load_pair(1, 2)
        load_pw(0)
        load_chunk(0, 1, 0)
        load_pair(1, 3)
        load_chunk(0, 1, 1)
        load_pw(1)
        load_chunk(1, 1, 0)
        load_chunk(1, 1, 1)
        load_pw(2)
        load_chunk(0, 2, 0)
        ident = const.tile([P, P], F32, name="ident")
        make_identity(nc, ident[:])
        identb = const.tile([P, P], BF16, name="identb")
        make_identity(nc, identb[:])
        eps = const.tile([P, 1], F32, name="eps")
        nc.vector.memset(eps[:], LN_EPS)
        warm = const.tile([P, 1], F32, name="warm")
        nc.scalar.activation(out=warm[:], in_=eps[:], func=ACT.Abs_reciprocal_sqrt, bias=eps[:], scale=1.0)
        sel = const.tile([P, 2 * NB, P], BF16, name="sel")
        for r in range(2 * NB):
            nc.vector.tensor_copy(out=sel[:, r, :], in_=identb[:, r : r + 1].to_broadcast([P, P]))
        g_all = const.tile([P, NB, D], BF16, name="g_all")
        junk2 = const.tile([P, 2], F32, name="junk2")

        def spread_first(row, lo, hi, pool, tag, on_vector):
            ps = pool.tile([P, H], F32, name="bc", tag=tag)
            nc.tensor.matmul(ps[:, 0 : hi - lo], lhsT=sel[:, row, :], rhs=gb[:, lo:hi], start=True, stop=True)
            dst = g_all[:, 0, lo:hi] if row == 0 else b_all[:, 0, lo - CUT : hi - CUT]
            if on_vector:
                nc.vector.tensor_copy(out=dst, in_=ps[:, 0 : hi - lo])
            else:
                nc.scalar.copy(out=dst, in_=ps[:, 0 : hi - lo])

        def spread(n):
            nc.sync.dma_start(out=g_all[:, n, :], in_=pln_g[n, :].partition_broadcast(P))
            nc.sync.dma_start(out=b_all[:, n, :], in_=pln_b[n, CUT:D].partition_broadcast(P))

        def code_tiles(op, n):
            if (op, n) not in codes:
                cd = codep.tile([P, 2 * D], U32, name="cd%d_%d" % (op, n), tag="cd%d" % op, align_bytes=64)
                sc = codep.tile([P, 2 * D], U8, name="sc%d_%d" % (op, n), tag="sc%d" % op, align_bytes=64)
                codes[(op, n)] = (cd, sc)
            return codes[(op, n)]

        def unit_source(u):
            if u[0] == "w":
                words = raw[(0, u[1], u[2])][:].bitcast(F32)
                starts = [[H * (2 * h + tl) + 256 * u[3] for tl in range(2)] for h in range(2)]
            elif u[0] == "a" and u[1] > 0:
                words = raw[(1, u[1], u[2] // 2)][:].bitcast(F32)
                starts = [[H * (2 * (u[2] % 2) + h) + 256 * g for g in range(2)] for h in range(2)]
            else:
                words = raw[("h", 0 if u[0] == "w0" else 1, u[2])][:].bitcast(F32)
                starts = [[H * tl + 256 * g for tl in range(2)] for g in range(2)]
                if u[0] == "a":
                    starts = [[H * tl + 256 * g for g in range(2)] for tl in range(2)]
            return words, starts

        def turn(u, h, home):
            pool, tag = tr_homes[home]
            words, starts = unit_source(u)
            if h == 0:
                unit[u] = grpp.tile([P, 2048], BF16, name="grp", tag="grp", align_bytes=64)
            ps = pool.tile([P, 2, 2, P], F32, name="tr", tag=tag)
            for tl in range(2):
                for w in range(2):
                    col = starts[h][tl]
                    nc.tensor.transpose(ps[:, tl, w, :], words[:, col + w : col + 256 : 2], ident[:])
            turned[(u, h)] = ps

        def gather(u, h, on_vector):
            src = turned[(u, h)][:].rearrange("p a w r -> p a r w")
            dst = unit[u][:].bitcast(F32).rearrange("p (a r w) -> p a r w", a=4, w=2)[:, 2 * h : 2 * h + 2]
            if on_vector:
                nc.vector.tensor_copy(out=dst, in_=src)
            else:
                nc.scalar.copy(out=dst, in_=src)

        def unit_front(u, home, v_copies):
            for h in range(2):
                turn(u, h, home)
                gather(u, h, h in v_copies)

        def quantize(op, n, cols, in_):
            cd, sc = code_tiles(op, n)
            nc.vector.quantize_mx(out=cd[:, cols].bitcast(FP8X4), scales=sc[:, cols], in_=in_)

        def unit_back(u):
            grp = unit[u]
            if u[0] == "w":
                lo = D * u[3] + H * u[2]
                quantize(0, u[1], slice(lo, lo + H), grp[:])
            elif u[0] == "a":
                quantize(1, u[1], slice(H * u[2], H * u[2] + H), grp[:])
            else:
                for g in range(2):
                    lo = D * g + 256 * u[2]
                    quantize(0, 0, slice(lo, lo + 256), grp[:, D * g : D * g + D])

        def make_cb(s):
            n = s // 8
            k, tl = divmod(s, 4)
            c_t = cbpool.tile([P, D - CUT], F32, name="cb%d" % s, tag="cb")
            nc.gpsimd.tensor_tensor(
                out=c_t[:], in0=pw_raw[k][:, tl * D + CUT : (tl + 1) * D], in1=b_all[:, n, :], op=ALU.add
            )
            cb_tiles[s] = c_t

        def make_c_pe(s):
            n = s // 8
            k, tl = divmod(s, 4)
            c_ps = psum_c.tile([P, CUT], F32, name="cps", tag="cps")
            nc.tensor.matmul(c_ps[:], lhsT=identb[:], rhs=pw_raw[k][:, tl * D : tl * D + CUT], start=True, stop=False)
            nc.tensor.matmul(c_ps[:], lhsT=sel[:, NB + n, :], rhs=gb[:, 0:CUT], start=False, stop=True)
            cps_tiles[s] = c_ps

        def finish_b(s):
            t_t, rstd = state[s]
            nc.vector.scalar_tensor_tensor(
                out=t_t[:, CUT:D], in0=t_t[:, CUT:D], scalar=rstd[:], in1=cb_tiles[s][:], op0=ALU.mult, op1=ALU.add
            )

        def finish_a(s):
            t_t, rstd = state[s]
            c_a = cps_tiles[s]
            nc.vector.scalar_tensor_tensor(
                out=t_t[:, 0:CUT], in0=t_t[:, 0:CUT], scalar=rstd[:], in1=c_a[:], op0=ALU.mult, op1=ALU.add
            )

        def finish(s, wide_first):
            parts = (finish_b, finish_a) if wide_first else (finish_a, finish_b)
            for part in parts:
                part(s)

        def store(s):
            n, i = divmod(s, 8)
            nc.sync.dma_start(out=out_view[n][:, i, :], in_=state[s][0][:])

        def mx(out, s, cols, g):
            n, i = divmod(s, 8)
            cd_w, sc_w = codes[(0, n)]
            cd_a, sc_a = codes[(1, n)]
            lo = H * (i // 2) + 256 * (i % 2) + P * g
            rows = slice(lo, lo + P)
            return dict(
                out=out,
                lhsT=cd_a[:, rows].bitcast(FP8X4),
                lhsT_scale=sc_a[:, rows],
                rhs=cd_w[:, cols].bitcast(FP8X4),
                rhs_scale=sc_w[:, cols],
            )

        def fold(s):
            f_ps = psum_s.tile([P, P], F32, name="f", tag="f")
            for g in range(2):
                for j in range(8):
                    cols = slice(D * g + P * j, D * g + P * j + P)
                    nc.tensor.matmul_mx(**mx(f_ps[:], s, cols, g), start=(g == 0 and j == 0), stop=(g == 1 and j == 7))
            x_tiles[(s, "f")] = f_ps

        def multiply(s, h):
            x_h = psum_x.tile([P, H], F32, name="x", tag="x")
            for g in range(2):
                cols = slice(D * g + H * h, D * g + H * h + H)
                nc.tensor.matmul_mx(**mx(x_h[:], s, cols, g), start=(g == 0), stop=(g == 1))
            x_tiles[(s, h)] = x_h

        def product(s):
            if FOLDS(s):
                fold(s)
            multiply(s, 0)
            multiply(s, 1)

        def settle(due):
            if due is not None:
                s, part, ssq = due
                state[s] = (state[s][0], make_rstd(s, part, ssq))

        def take_sums(s, due):
            if FOLDS(s):
                return
            sums = smallp.tile([P, 2], F32, name="sums%d" % s, tag="sums")
            for h in range(2):
                junk = junkp.tile([P, H], BF16, name="junk", tag="junk")
                nc.scalar.activation(out=junk[:], in_=x_tiles[(s, h)][:], func=ACT.Copy, accum_out=sums[:, h : h + 1])
                if h == 0:
                    settle(due)
            all_sums[s] = sums

        def take_mean(s):
            negmean = smallp.tile([P, 1], F32, name="nm%d" % s, tag="nm")
            if FOLDS(s):
                junk = junkp.tile([P, H], BF16, name="junk", tag="junk")
                nc.scalar.activation(
                    out=junk[:, 0:P], in_=x_tiles[(s, "f")][:], func=ACT.Copy, scale=-1.0 / D, accum_out=negmean[:]
                )
            else:
                nc.scalar.activation(
                    out=junk2[:], in_=all_sums[s][:], func=ACT.Copy, scale=-1.0 / D, accum_out=negmean[:]
                )
            negmeans[s] = negmean

        def take_squares(s):
            out = []
            for h in range(2):
                junk = junkp.tile([P, H], BF16, name="junk", tag="junk")
                ssq = smallp.tile([P, 1], F32, name="ssq%d_%d" % (s, h), tag="ssq%d" % h)
                nc.scalar.activation(
                    out=junk[:], in_=x_tiles[(s, h)][:], func=ACT.Square, bias=negmeans[s][:], scale=1.0, accum_out=ssq[:]
                )
                out.append(ssq)
            part = smallp.tile([P, 1], F32, name="part%d" % s, tag="part")
            nc.scalar.activation(out=part[:], in_=out[0][:], func=ACT.Identity, bias=eps[:], scale=1.0 / D)
            return part, out[1]

        def make_rstd(s, part, ssq):
            rstd = smallp.tile([P, 1], F32, name="rstd%d" % s, tag="rstd")
            nc.scalar.activation(out=rstd[:], in_=ssq[:], func=ACT.Abs_reciprocal_sqrt, bias=part[:], scale=1.0 / D)
            return rstd

        def scale_g(s):
            t_t = tpool.tile([P, D], F32, name="t%d" % s, tag="t")
            for h in range(2):
                cols = slice(H * h, H * h + H)
                nc.vector.scalar_tensor_tensor(
                    out=t_t[:, cols], in0=x_tiles[(s, h)][:], scalar=negmeans[s][:], in1=g_all[:, s // 8, cols],
                    op0=ALU.add, op1=ALU.mult,
                )
            return t_t

        head = [("w0", 0, q) for q in range(4)]
        first = ("a", 0, 0)
        for k, u in enumerate(head):
            unit_front(u, k % 3, ((1,) if k == 1 else ()))
            if k > 0:
                unit_back(head[k - 1])
        turn(first, 0, 1)
        gather(first, 0, False)
        unit_back(head[-1])
        quantize(1, 0, slice(0, 256), unit[first][:, 0:D])
        turn(first, 1, 1)
        gather(first, 1, False)
        for lo in (0, H):
            spread_first(0, lo, lo + H, psum_x, "x", lo == 0)
        spread_first(NB, CUT, H, psum_s, "f", False)
        spread_first(NB, H, D, psum_c, "cps", True)
        quantize(1, 0, slice(256, H), unit[first][:, D : 2 * D])
        product(0)
        product(1)
        make_cb(0)
        units = prep_units()
        for h in range(2):
            turn(units[0], h, 0)
        waiting = []

        due = None
        for s in range(N_SLOTS):
            n, i = divmod(s, 8)
            last = s + 1 == N_SLOTS
            new_units = units[0:2] if s == 0 else units[s + 1 : s + 2]
            v_copies = ((1,) if s % 6 == 1 else ())
            for u in new_units:
                if u != units[0]:
                    for h in range(2):
                        turn(u, h, 3 + h if s == 0 else 0)
            take_sums(s, due)
            if s > 0 and not FOLDS(s):
                for u in new_units:
                    gather(u, 0, 0 in v_copies)
            take_mean(s)
            if FOLDS(s):
                settle(due)
            part, ssq = take_squares(s)
            for u in waiting:
                unit_back(u)
            if s > 0:
                make_c_pe(s - 1)
                finish(s - 1, bool(waiting))
                store(s - 1)
            if not last:
                make_cb(s + 1)
            if s > 0:
                for u in new_units:
                    if FOLDS(s):
                        gather(u, 0, 0 in v_copies)
                    gather(u, 1, 1 in v_copies)
            for u in new_units:
                if u[0] == "w" and u[3] == 1 and u[1] == 1:
                    load_chunk(*((0, 2, 1) if u[2] == 0 else (1, 2, 0)))
                if u == ("a", 1, 1):
                    load_chunk(1, 2, 1)
            t_t = scale_g(s)
            if s == 0:
                for u in new_units:
                    gather(u, 0, u == units[0])
                    gather(u, 1, True)
            state[s] = (t_t, None)
            due = (s, part, ssq)
            if s > 0 and not last:
                product(s + 1)
            waiting = new_units
            if s in (1, 8):
                spread(1 if s == 1 else 2)
            if s >= 4 and s % 4 == 0 and s // 4 + 2 < 2 * NB:
                load_pw(s // 4 + 2)
        settle(due)
        make_c_pe(N_SLOTS - 1)
        finish_a(N_SLOTS - 1)
        nc.sync.dma_start(out=out_view[NB - 1][:, 7, 0:CUT], in_=state[N_SLOTS - 1][0][:, 0:CUT])
        finish_b(N_SLOTS - 1)
        nc.sync.dma_start(out=out_view[NB - 1][:, 7, CUT:D], in_=state[N_SLOTS - 1][0][:, CUT:D])
